import numpy as np
import ml_dtypes


def mxq(x, axis, fmt="e4m3"):
    dtype, down = {"e4m3": (ml_dtypes.float8_e4m3fn, 7), "e5m2": (ml_dtypes.float8_e5m2, 14)}[fmt]
    v = np.moveaxis(np.asarray(x, np.float32).astype(ml_dtypes.bfloat16).astype(np.float64), axis, -1)
    blocks = v.reshape(v.shape[:-1] + (-1, 32))
    amax = np.abs(blocks).max(-1, keepdims=True)
    byte = np.maximum(np.where(amax > 0, np.frexp(amax)[1] - 1 + 127, 0) - down, 1)
    scale = np.exp2(byte - 127.0)
    codes = (blocks / scale).astype(np.float32).astype(dtype).astype(np.float64)
    return np.moveaxis((codes * scale).reshape(v.shape), -1, axis)


WIDE = False


def mx_kscale(k):
    if not WIDE:
        return np.ones(k)
    levels = np.array([10, -10, 5, -5, 0])
    a = np.random.permutation(np.resize(levels, k // 512 * 4)).reshape(k // 512, 4)
    idx = np.arange(k)
    return np.exp2(a[idx // 512, idx % 128 // 32])


BF16 = ml_dtypes.bfloat16


def bf(x):
    return np.asarray(x, np.float32).astype(BF16)


def f64(x):
    return np.asarray(x).astype(np.float64)


E2M1 = np.array([0.0, 0.5, 1.0, 1.5, 2.0, 3.0, 4.0, 6.0, -0.0, -0.5, -1.0, -1.5, -2.0, -3.0, -4.0, -6.0])


def pack_weight(w, fmt):
    k, n = w.shape
    w = f64(bf(w)).reshape(k // 32, 32, n)
    amax = np.abs(w).max(1)
    if fmt == "e4m3":
        byte = np.frexp(amax)[1] - 1 + 127 - 7
    else:
        mant, ex = np.frexp(amax / 6.0)
        byte = np.where(mant > 0.5, ex, ex - 1) + 127
    byte = np.clip(np.where(amax > 0, byte, 1), 1, 254)
    scaled = (w * np.exp2(127.0 - byte)[:, None, :]).reshape(k, n).astype(np.float32)
    by_word = np.ascontiguousarray(scaled.reshape(k // 512, 128, 4, n).transpose(0, 1, 3, 2))
    if fmt == "e4m3":
        words = by_word.astype(ml_dtypes.float8_e4m3fn).view(np.uint8)
    else:
        c = by_word.astype(ml_dtypes.float4_e2m1fn).view(np.uint8) & 0xF
        words = c[..., 0::2] | (c[..., 1::2] << 4)
    return np.ascontiguousarray(words), np.ascontiguousarray(byte.astype(np.uint8).reshape(k // 512, 16, n))


def unpack_weight(words, scales, fmt):
    g, p, n, _ = words.shape
    if fmt == "e4m3":
        vals = np.ascontiguousarray(words).view(ml_dtypes.float8_e4m3fn).astype(np.float64)
    else:
        nib = np.empty((g, p, n, 4), np.uint8)
        nib[..., 0::2] = words & 0xF
        nib[..., 1::2] = words >> 4
        vals = E2M1[nib]
    vals = vals * np.repeat(np.exp2(scales.astype(np.float64) - 127.0), 8, axis=1)[..., None]
    return vals.transpose(0, 1, 3, 2).reshape(g * 512, n)

def pack4(w):
    words, scales = pack_weight(w, "e2m1")
    return words.reshape(words.shape[0], 128, -1), scales


def unpack4(words, scales):
    return unpack_weight(words.reshape(words.shape[0], 128, -1, 2), scales, "e2m1")


B, T, D, H, KV, DH = 4, 2048, 1024, 2, 1, 32
G = H // KV
HALF = DH // 2
ROPE_THETA = 1e6
YARN_FACTOR = 64.0
ORIG_MAX_POS = 4096.0
BETA_FAST, BETA_SLOW = 4.0, 1.0
ATTN_FACTOR = 0.1 * np.log(YARN_FACTOR) + 1.0


def corr_dim(num_rot):
    return DH * np.log(ORIG_MAX_POS / (num_rot * 2 * np.pi)) / (2 * np.log(ROPE_THETA))


def yarn_inv_freq():
    low = float(np.sum(np.arange(DH) + 1 <= corr_dim(BETA_FAST)))
    high = min(float(np.sum(np.arange(DH) < corr_dim(BETA_SLOW))), DH - 1.0)
    if low == high:
        high += 0.001
    ramp = np.clip((np.arange(HALF) - low) / (high - low), 0.0, 1.0)
    pos_freqs = ROPE_THETA ** (np.arange(0, DH, 2) / DH)
    inv_extrap = 1.0 / pos_freqs
    inv_interp = 1.0 / (YARN_FACTOR * pos_freqs)
    extrap_factor = 1.0 - ramp
    return inv_interp * (1.0 - extrap_factor) + inv_extrap * extrap_factor


def rope_yarn(v):
    angles = np.arange(T)[:, None] * yarn_inv_freq()[None, :]
    cos = np.cos(angles)[None, :, None, :]
    sin = np.sin(angles)[None, :, None, :]
    v_even = v[..., 0::2]
    v_odd = v[..., 1::2]
    out_even = v_even * cos - v_odd * sin
    out_odd = v_even * sin + v_odd * cos
    return np.stack([out_even, out_odd], axis=-1).reshape(v.shape) * ATTN_FACTOR


def setup_inputs():
    s = mx_kscale(D)
    x = bf(np.random.standard_normal((B, T, D)) * s)
    words, scales = pack4(np.random.standard_normal((D, (H + 2 * KV) * DH)) / np.sqrt(D) / s[:, None])
    return {"x": x, "w_qkv_words": words, "w_qkv_scales": scales}


def reference(x, w_qkv_words, w_qkv_scales):
    qkv = mxq(f64(x), 2, "e4m3") @ unpack4(w_qkv_words, w_qkv_scales)
    q = qkv[:, :, :H * DH].reshape(B, T, H, DH)
    k = qkv[:, :, H * DH:(H + KV) * DH].reshape(B, T, KV, DH)
    v = qkv[:, :, (H + KV) * DH:].reshape(B, T, KV, DH)
    q = rope_yarn(q)
    k = rope_yarn(k)
    q = q.reshape(B, T, KV, G, DH).transpose(0, 2, 3, 1, 4)
    k = k.transpose(0, 2, 1, 3)
    v = v.transpose(0, 2, 1, 3)
    return q, k, v

@@ -1,0 +1,260 @@
+import math
+from contextlib import ExitStack
+
+import concourse.mybir as mybir
+from concourse.masks import make_identity
+
+F32 = mybir.dt.float32
+BF16 = mybir.dt.bfloat16
+I32 = mybir.dt.int32
+U32 = mybir.dt.uint32
+U8 = mybir.dt.uint8
+FP8X4 = mybir.dt.float8_e4m3fn_x4
+FP4X4 = mybir.dt.float4_e2m1fn_x4
+ALU = mybir.AluOpType
+ACT = mybir.ActivationFunctionType
+
+BATCH, T, D = 4, 2048, 1024
+DH = 32
+HALF = DH // 2
+ROPED_HEADS = 3
+HEADS = 4
+COLS = HEADS * DH
+
+P = 128
+K_PASS = 4 * P
+PASSES = D // K_PASS
+WORDS_PASS = K_PASS // 2
+
+TILES_BATCH = T // P
+GROUP = 4
+GROUPS_BATCH = TILES_BATCH // GROUP
+GROUPS = BATCH * GROUPS_BATCH
+STORE_GROUPS = 2
+STORE_TILES = STORE_GROUPS * GROUP
+
+ROPE_THETA = 1e6
+YARN_FACTOR = 64.0
+RAMP_LOW, RAMP_HIGH = 5, 8
+ATTN_FACTOR = 0.1 * math.log(YARN_FACTOR) + 1.0
+
+ROUND = 1.5 * 2.0**23
+
+FLOPS = 2 * BATCH * T * D * COLS
+
+
+def turns_per_position(i):
+    plain = ROPE_THETA ** (-i / HALF)
+    ramp = min(max((i - RAMP_LOW) / (RAMP_HIGH - RAMP_LOW), 0.0), 1.0)
+    return (plain * (1.0 - ramp) + plain / YARN_FACTOR * ramp) / (2.0 * math.pi)
+
+
+def split_13_bits(value):
+    exponent = math.floor(math.log(value) / math.log(2.0))
+    step = 2.0 ** (exponent - 12)
+    high = round(value / step) * step
+    return high, value - high
+
+
+def tile_causalselfattentiongqa_pa_t_kernel(tc, x, w_qkv_words, w_qkv_scales, out_0, out_1, out_2):
+    nc = tc.nc
+    with ExitStack() as ctx:
+        const = ctx.enter_context(tc.tile_pool(name="const", bufs=1))
+        x_pool = ctx.enter_context(tc.tile_pool(name="x", bufs=GROUPS))
+        grouped_pool = ctx.enter_context(tc.tile_pool(name="grouped", bufs=3))
+        mx_pool = ctx.enter_context(tc.tile_pool(name="mx", bufs=3))
+        work = ctx.enter_context(tc.tile_pool(name="work", bufs=2))
+        out_pool = ctx.enter_context(tc.tile_pool(name="out", bufs=3))
+        xt_pool = ctx.enter_context(tc.psum_pool(name="xt", bufs=6))
+        acc_pool = ctx.enter_context(tc.psum_pool(name="acc", bufs=2))
+        ctx.enter_context(tc.manual_schedule())
+
+        x_tiles = []
+
+        def load_group(i):
+            batch, part = divmod(i, GROUPS_BATCH)
+            x_sb = x_pool.tile([P, GROUP, D], BF16)
+            tokens = x[batch].rearrange("(p a) k -> p a k", a=TILES_BATCH)
+            nc.sync.dma_start(out=x_sb[:], in_=tokens[:, part * GROUP : (part + 1) * GROUP, :])
+            x_tiles.append(x_sb)
+
+        w_words = const.tile([P, PASSES, 2 * COLS], U8, align_bytes=64)
+        w_planes = const.tile([P, PASSES, COLS], U8, align_bytes=64)
+        nc.vector.memset(w_planes[:].bitcast(I32), 0)
+
+        load_group(0)
+        nc.sync.dma_start(out=w_words[:].bitcast(I32), in_=w_qkv_words.rearrange("g p n -> p g n").bitcast(I32))
+        for quadrant in range(4):
+            nc.sync.dma_start(
+                out=w_planes[32 * quadrant : 32 * quadrant + 4].bitcast(I32),
+                in_=w_qkv_scales[:, 4 * quadrant : 4 * quadrant + 4, :].rearrange("g r n -> r g n").bitcast(I32),
+            )
+        for i in range(1, GROUPS):
+            load_group(i)
+
+        position_int = const.tile([P, TILES_BATCH], I32)
+        nc.gpsimd.iota(position_int[:], pattern=[[1, TILES_BATCH]], base=0, channel_multiplier=TILES_BATCH)
+        identity = const.tile([P, P], F32)
+        make_identity(nc, identity[:])
+
+        zero = const.tile([P, 1], F32)
+        nc.vector.memset(zero[:], 0.0)
+        sin_of_zero = const.tile([P, 1], F32)
+        nc.scalar.activation(out=sin_of_zero[:], in_=zero[:], func=ACT.Sin)
+
+        angle_shape = [P, TILES_BATCH, HALF]
+        position = const.tile([P, TILES_BATCH], F32)
+        nc.vector.tensor_copy(out=position[:], in_=position_int[:])
+
+        def minus_fraction(out, value, shifted):
+            nc.vector.tensor_scalar_add(out=shifted, in0=value, scalar1=ROUND)
+            nc.vector.scalar_tensor_tensor(
+                out=out, in0=shifted, scalar=ROUND, in1=value, op0=ALU.subtract, op1=ALU.subtract
+            )
+
+        coarse = const.tile(angle_shape, F32)
+        for i in range(HALF):
+            high, low = split_13_bits(turns_per_position(i))
+            nc.vector.tensor_scalar_mul(out=coarse[:, :, i], in0=position[:], scalar1=high)
+        coarse_shifted = const.tile(angle_shape, F32)
+        minus_coarse = const.tile(angle_shape, F32)
+        minus_fraction(minus_coarse[:], coarse[:], coarse_shifted[:])
+
+        turns = const.tile(angle_shape, F32)
+        for i in range(HALF):
+            high, low = split_13_bits(turns_per_position(i))
+            nc.vector.scalar_tensor_tensor(
+                out=turns[:, :, i], in0=position[:], scalar=low, in1=minus_coarse[:, :, i],
+                op0=ALU.mult, op1=ALU.subtract,
+            )
+        turns_shifted = const.tile(angle_shape, F32)
+        minus_turns = const.tile(angle_shape, F32)
+        minus_fraction(minus_turns[:], turns[:], turns_shifted[:])
+
+        minus_abs = const.tile(angle_shape, F32)
+        nc.vector.scalar_tensor_tensor(
+            out=minus_abs[:], in0=minus_turns[:], scalar=-1.0, in1=minus_turns[:], op0=ALU.mult, op1=ALU.min
+        )
+        quarter_less_abs = const.tile(angle_shape, F32)
+        nc.vector.tensor_scalar_add(out=quarter_less_abs[:], in0=minus_abs[:], scalar1=0.25)
+
+        table_of_even = const.tile([P, TILES_BATCH, HALF, 2], F32)
+        table_of_odd = const.tile([P, TILES_BATCH, HALF, 2], F32)
+
+        def build_tables():
+            sin = const.tile(angle_shape, F32)
+            cos = const.tile(angle_shape, F32)
+            nc.scalar.activation(out=sin[:], in_=minus_turns[:], func=ACT.Sin, scale=-2.0 * math.pi)
+            nc.scalar.activation(out=cos[:], in_=quarter_less_abs[:], func=ACT.Sin, scale=2.0 * math.pi)
+            nc.vector.tensor_scalar_mul(out=table_of_even[:, :, :, 0], in0=cos[:], scalar1=ATTN_FACTOR)
+            nc.vector.tensor_scalar_mul(out=table_of_even[:, :, :, 1], in0=sin[:], scalar1=ATTN_FACTOR)
+            nc.vector.tensor_scalar_mul(out=table_of_odd[:, :, :, 0], in0=sin[:], scalar1=-ATTN_FACTOR)
+            nc.vector.tensor_scalar_mul(out=table_of_odd[:, :, :, 1], in0=cos[:], scalar1=ATTN_FACTOR)
+
+        grouped_tiles = {}
+        code_tiles = {}
+        plane_tiles = {}
+        acc_tiles = {}
+        result_tiles = {}
+
+        def transpose_group(i):
+            grouped = grouped_pool.tile([P, GROUP * D], BF16, align_bytes=64)
+            grouped_words = grouped[:].bitcast(F32).rearrange(
+                "p (j g r u) -> p j g r u", j=GROUP, g=PASSES, u=2
+            )
+            for j in range(GROUP):
+                x_words = x_tiles[i][:, j, :].bitcast(F32)
+                xt = xt_pool.tile([P, PASSES, 2, P], F32)
+                for g in range(PASSES):
+                    for u in range(2):
+                        first = WORDS_PASS * g + u
+                        nc.tensor.transpose(xt[:, g, u, :], x_words[:, first : WORDS_PASS * (g + 1) : 2], identity[:])
+                nc.scalar.copy(out=grouped_words[:, j], in_=xt[:].rearrange("p g u r -> p g r u"))
+            grouped_tiles[i] = grouped
+
+        def quantise_group(i):
+            codes = mx_pool.tile([P, GROUP, PASSES, P], U32, align_bytes=64)
+            planes = mx_pool.tile([P, GROUP, PASSES, P], U8, align_bytes=64)
+            for j in range(GROUP):
+                nc.vector.quantize_mx(
+                    out=codes[:, j].rearrange("p g r -> p (g r)").bitcast(FP8X4),
+                    scales=planes[:, j].rearrange("p g r -> p (g r)"),
+                    in_=grouped_tiles[i][:, j * D : (j + 1) * D],
+                )
+            code_tiles[i] = codes
+            plane_tiles[i] = planes
+
+        def multiply_group(i):
+            acc = acc_pool.tile([P, GROUP, COLS], F32)
+            for j in range(GROUP):
+                for g in range(PASSES):
+                    nc.tensor.matmul_mx(
+                        out=acc[:, j, :],
+                        lhsT=code_tiles[i][:, j, g, :].bitcast(FP8X4),
+                        lhsT_scale=plane_tiles[i][:, j, g, :],
+                        rhs=w_words[:, g, :].bitcast(FP4X4),
+                        rhs_scale=w_planes[:, g, :],
+                        start=(g == 0),
+                        stop=(g == PASSES - 1),
+                    )
+            acc_tiles[i] = acc
+
+        def rope_group(i):
+            store, place = divmod(i, STORE_GROUPS)
+            if place == 0:
+                result = out_pool.tile([P, HEADS, STORE_TILES, DH], F32)
+                result_tiles[store] = result
+            result = result_tiles[store]
+            here = slice(place * GROUP, (place + 1) * GROUP)
+            first_tile = (i % GROUPS_BATCH) * GROUP
+            acc = acc_tiles[i]
+
+            pair_shape = [P, GROUP, ROPED_HEADS, HALF, 2]
+            pairs = acc[:, :, 0 : ROPED_HEADS * DH].rearrange("p j (h i two) -> p j h i two", h=ROPED_HEADS, two=2)
+            tiles_here = slice(first_tile, first_tile + GROUP)
+            from_even = work.tile(pair_shape, F32)
+            nc.vector.tensor_tensor(
+                out=from_even[:],
+                in0=pairs[:, :, :, :, 0:1].to_broadcast(pair_shape),
+                in1=table_of_even[:, tiles_here].unsqueeze(2).to_broadcast(pair_shape),
+                op=ALU.mult,
+            )
+            from_odd = work.tile(pair_shape, F32)
+            nc.vector.tensor_tensor(
+                out=from_odd[:],
+                in0=pairs[:, :, :, :, 1:2].to_broadcast(pair_shape),
+                in1=table_of_odd[:, tiles_here].unsqueeze(2).to_broadcast(pair_shape),
+                op=ALU.mult,
+            )
+            nc.vector.tensor_copy(out=result[:, ROPED_HEADS, here, :], in_=acc[:, :, ROPED_HEADS * DH : COLS])
+            nc.vector.tensor_tensor(
+                out=result[:, 0:ROPED_HEADS, here, :],
+                in0=from_even[:].rearrange("p j h i two -> p h j (i two)"),
+                in1=from_odd[:].rearrange("p j h i two -> p h j (i two)"),
+                op=ALU.add,
+            )
+
+            if place == STORE_GROUPS - 1:
+                batch, part = divmod(store, GROUPS_BATCH // STORE_GROUPS)
+                stored = slice(part * STORE_TILES, (part + 1) * STORE_TILES)
+                q_rows = out_0[batch, 0].rearrange("h (p a) d -> p h a d", a=TILES_BATCH)
+                k_rows = out_1[batch, 0].rearrange("(p a) d -> p a d", a=TILES_BATCH)
+                v_rows = out_2[batch, 0].rearrange("(p a) d -> p a d", a=TILES_BATCH)
+                nc.sync.dma_start(out=q_rows[:, :, stored, :], in_=result[:, 0:2, :, :])
+                nc.sync.dma_start(out=k_rows[:, stored, :], in_=result[:, 2, :, :])
+                nc.sync.dma_start(out=v_rows[:, stored, :], in_=result[:, 3, :, :])
+
+        transpose_group(0)
+        quantise_group(0)
+        build_tables()
+        transpose_group(1)
+        quantise_group(1)
+        multiply_group(0)
+        for i in range(2, GROUPS):
+            transpose_group(i)
+            rope_group(i - 2)
+            quantise_group(i)
+            multiply_group(i - 1)
+        rope_group(GROUPS - 2)
+        multiply_group(GROUPS - 1)
+        rope_group(GROUPS - 1)

@@ -30,6 +30,8 @@ TILES_BATCH = T // P
 GROUP = 4
 GROUPS_BATCH = TILES_BATCH // GROUP
 GROUPS = BATCH * GROUPS_BATCH
+LOAD_TILES = 2
+LOADS = BATCH * TILES_BATCH // LOAD_TILES
 STORE_GROUPS = 2
 STORE_TILES = STORE_GROUPS * GROUP
 
@@ -60,37 +62,39 @@ def tile_causalselfattentiongqa_pa_t_kernel(tc, x, w_qkv_words, w_qkv_scales, ou
     nc = tc.nc
     with ExitStack() as ctx:
         const = ctx.enter_context(tc.tile_pool(name="const", bufs=1))
-        x_pool = ctx.enter_context(tc.tile_pool(name="x", bufs=GROUPS))
+        x_pool = ctx.enter_context(tc.tile_pool(name="x", bufs=LOADS))
         grouped_pool = ctx.enter_context(tc.tile_pool(name="grouped", bufs=3))
         mx_pool = ctx.enter_context(tc.tile_pool(name="mx", bufs=3))
         work = ctx.enter_context(tc.tile_pool(name="work", bufs=2))
-        out_pool = ctx.enter_context(tc.tile_pool(name="out", bufs=3))
+        out_pool = ctx.enter_context(tc.tile_pool(name="out", bufs=GROUPS // STORE_GROUPS))
         xt_pool = ctx.enter_context(tc.psum_pool(name="xt", bufs=6))
         acc_pool = ctx.enter_context(tc.psum_pool(name="acc", bufs=2))
         ctx.enter_context(tc.manual_schedule())
 
         x_tiles = []
 
-        def load_group(i):
-            batch, part = divmod(i, GROUPS_BATCH)
-            x_sb = x_pool.tile([P, GROUP, D], BF16)
+        def load_x(n):
+            batch, part = divmod(n, TILES_BATCH // LOAD_TILES)
+            x_sb = x_pool.tile([P, LOAD_TILES, D], BF16)
             tokens = x[batch].rearrange("(p a) k -> p a k", a=TILES_BATCH)
-            nc.sync.dma_start(out=x_sb[:], in_=tokens[:, part * GROUP : (part + 1) * GROUP, :])
+            nc.sync.dma_start(out=x_sb[:], in_=tokens[:, part * LOAD_TILES : (part + 1) * LOAD_TILES, :])
             x_tiles.append(x_sb)
 
         w_words = const.tile([P, PASSES, 2 * COLS], U8, align_bytes=64)
         w_planes = const.tile([P, PASSES, COLS], U8, align_bytes=64)
         nc.vector.memset(w_planes[:].bitcast(I32), 0)
 
-        load_group(0)
+        loads_before_w = 2 * GROUP // LOAD_TILES
+        for n in range(loads_before_w):
+            load_x(n)
         nc.sync.dma_start(out=w_words[:].bitcast(I32), in_=w_qkv_words.rearrange("g p n -> p g n").bitcast(I32))
         for quadrant in range(4):
             nc.sync.dma_start(
                 out=w_planes[32 * quadrant : 32 * quadrant + 4].bitcast(I32),
                 in_=w_qkv_scales[:, 4 * quadrant : 4 * quadrant + 4, :].rearrange("g r n -> r g n").bitcast(I32),
             )
-        for i in range(1, GROUPS):
-            load_group(i)
+        for n in range(loads_before_w, LOADS):
+            load_x(n)
 
         position_int = const.tile([P, TILES_BATCH], I32)
         nc.gpsimd.iota(position_int[:], pattern=[[1, TILES_BATCH]], base=0, channel_multiplier=TILES_BATCH)
@@ -163,7 +167,8 @@ def tile_causalselfattentiongqa_pa_t_kernel(tc, x, w_qkv_words, w_qkv_scales, ou
                 "p (j g r u) -> p j g r u", j=GROUP, g=PASSES, u=2
             )
             for j in range(GROUP):
-                x_words = x_tiles[i][:, j, :].bitcast(F32)
+                load, place = divmod(i * GROUP + j, LOAD_TILES)
+                x_words = x_tiles[load][:, place, :].bitcast(F32)
                 xt = xt_pool.tile([P, PASSES, 2, P], F32)
                 for g in range(PASSES):
                     for u in range(2):

@@ -214,6 +214,8 @@ def tile_causalselfattentiongqa_pa_t_kernel(tc, x, w_qkv_words, w_qkv_scales, ou
             first_tile = (i % GROUPS_BATCH) * GROUP
             acc = acc_tiles[i]
 
+            nc.scalar.copy(out=result[:, ROPED_HEADS, here, :], in_=acc[:, :, ROPED_HEADS * DH : COLS])
+
             pair_shape = [P, GROUP, ROPED_HEADS, HALF, 2]
             pairs = acc[:, :, 0 : ROPED_HEADS * DH].rearrange("p j (h i two) -> p j h i two", h=ROPED_HEADS, two=2)
             tiles_here = slice(first_tile, first_tile + GROUP)
@@ -231,7 +233,6 @@ def tile_causalselfattentiongqa_pa_t_kernel(tc, x, w_qkv_words, w_qkv_scales, ou
                 in1=table_of_odd[:, tiles_here].unsqueeze(2).to_broadcast(pair_shape),
                 op=ALU.mult,
             )
-            nc.vector.tensor_copy(out=result[:, ROPED_HEADS, here, :], in_=acc[:, :, ROPED_HEADS * DH : COLS])
             nc.vector.tensor_tensor(
                 out=result[:, 0:ROPED_HEADS, here, :],
                 in0=from_even[:].rearrange("p j h i two -> p h j (i two)"),
@@ -256,8 +257,8 @@ def tile_causalselfattentiongqa_pa_t_kernel(tc, x, w_qkv_words, w_qkv_scales, ou
         quantise_group(1)
         multiply_group(0)
         for i in range(2, GROUPS):
-            transpose_group(i)
             rope_group(i - 2)
+            transpose_group(i)
             quantise_group(i)
             multiply_group(i - 1)
         rope_group(GROUPS - 2)

@@ -69,7 +69,6 @@ def tile_causalselfattentiongqa_pa_t_kernel(tc, x, w_qkv_words, w_qkv_scales, ou
         out_pool = ctx.enter_context(tc.tile_pool(name="out", bufs=GROUPS // STORE_GROUPS))
         xt_pool = ctx.enter_context(tc.psum_pool(name="xt", bufs=6))
         acc_pool = ctx.enter_context(tc.psum_pool(name="acc", bufs=2))
-        ctx.enter_context(tc.manual_schedule())
 
         x_tiles = []
 

@@ -28,12 +28,16 @@ WORDS_PASS = K_PASS // 2
 
 TILES_BATCH = T // P
 GROUP = 4
-GROUPS_BATCH = TILES_BATCH // GROUP
-GROUPS = BATCH * GROUPS_BATCH
-LOAD_TILES = 2
-LOADS = BATCH * TILES_BATCH // LOAD_TILES
-STORE_GROUPS = 2
-STORE_TILES = STORE_GROUPS * GROUP
+STORE_TILES = 16
+QUANT_TILES = 1
+
+BATCH_GROUPS = [4, 4, 4, 4]
+LAST_BATCH_GROUPS = [4, 4, 4, 4]
+BATCH_LOADS = [2, 2, 2, 2, 2, 2, 2, 2]
+FIRST_BATCH_LOADS = [2, 2, 2, 2, 2, 2, 2, 2]
+BATCH_STORES = [16]
+LAST_BATCH_STORES = [8, 4, 4]
+RESULT_BUFFERS = 4
 
 ROPE_THETA = 1e6
 YARN_FACTOR = 64.0
@@ -62,28 +66,44 @@ def tile_causalselfattentiongqa_pa_t_kernel(tc, x, w_qkv_words, w_qkv_scales, ou
     nc = tc.nc
     with ExitStack() as ctx:
         const = ctx.enter_context(tc.tile_pool(name="const", bufs=1))
-        x_pool = ctx.enter_context(tc.tile_pool(name="x", bufs=LOADS))
+        x_pool = ctx.enter_context(tc.tile_pool(name="x", bufs=1))
         grouped_pool = ctx.enter_context(tc.tile_pool(name="grouped", bufs=3))
         mx_pool = ctx.enter_context(tc.tile_pool(name="mx", bufs=3))
         work = ctx.enter_context(tc.tile_pool(name="work", bufs=2))
-        out_pool = ctx.enter_context(tc.tile_pool(name="out", bufs=GROUPS // STORE_GROUPS))
+        out_pool = ctx.enter_context(tc.tile_pool(name="out", bufs=RESULT_BUFFERS))
         xt_pool = ctx.enter_context(tc.psum_pool(name="xt", bufs=6))
         acc_pool = ctx.enter_context(tc.psum_pool(name="acc", bufs=2))
 
-        x_tiles = []
+        def spans(batch_plans):
+            found = []
+            for batch in range(BATCH):
+                first = 0
+                for tiles in batch_plans[batch]:
+                    found.append((batch, first, tiles))
+                    first += tiles
+                assert first == TILES_BATCH
+            return found
+
+        loads = spans([FIRST_BATCH_LOADS] + [BATCH_LOADS] * (BATCH - 1))
+        groups = spans([BATCH_GROUPS] * (BATCH - 1) + [LAST_BATCH_GROUPS])
+        stores = spans([BATCH_STORES] * (BATCH - 1) + [LAST_BATCH_STORES])
+        GROUPS = len(groups)
+
+        x_rows = {}
 
         def load_x(n):
-            batch, part = divmod(n, TILES_BATCH // LOAD_TILES)
-            x_sb = x_pool.tile([P, LOAD_TILES, D], BF16)
+            batch, first, tiles = loads[n]
+            x_sb = x_pool.tile([P, tiles, D], BF16, name="x%d" % n)
             tokens = x[batch].rearrange("(p a) k -> p a k", a=TILES_BATCH)
-            nc.sync.dma_start(out=x_sb[:], in_=tokens[:, part * LOAD_TILES : (part + 1) * LOAD_TILES, :])
-            x_tiles.append(x_sb)
+            nc.sync.dma_start(out=x_sb[:], in_=tokens[:, first : first + tiles, :])
+            for place in range(tiles):
+                x_rows[(batch, first + place)] = x_sb[:, place, :]
 
         w_words = const.tile([P, PASSES, 2 * COLS], U8, align_bytes=64)
         w_planes = const.tile([P, PASSES, COLS], U8, align_bytes=64)
         nc.vector.memset(w_planes[:].bitcast(I32), 0)
 
-        loads_before_w = 2 * GROUP // LOAD_TILES
+        loads_before_w = len([1 for batch, first, tiles in loads if batch == 0 and first < 2 * GROUP])
         for n in range(loads_before_w):
             load_x(n)
         nc.sync.dma_start(out=w_words[:].bitcast(I32), in_=w_qkv_words.rearrange("g p n -> p g n").bitcast(I32))
@@ -92,7 +112,7 @@ def tile_causalselfattentiongqa_pa_t_kernel(tc, x, w_qkv_words, w_qkv_scales, ou
                 out=w_planes[32 * quadrant : 32 * quadrant + 4].bitcast(I32),
                 in_=w_qkv_scales[:, 4 * quadrant : 4 * quadrant + 4, :].rearrange("g r n -> r g n").bitcast(I32),
             )
-        for n in range(loads_before_w, LOADS):
+        for n in range(loads_before_w, len(loads)):
             load_x(n)
 
         position_int = const.tile([P, TILES_BATCH], I32)
@@ -165,9 +185,9 @@ def tile_causalselfattentiongqa_pa_t_kernel(tc, x, w_qkv_words, w_qkv_scales, ou
             grouped_words = grouped[:].bitcast(F32).rearrange(
                 "p (j g r u) -> p j g r u", j=GROUP, g=PASSES, u=2
             )
-            for j in range(GROUP):
-                load, place = divmod(i * GROUP + j, LOAD_TILES)
-                x_words = x_tiles[load][:, place, :].bitcast(F32)
+            batch, first_tile, tiles = groups[i]
+            for j in range(tiles):
+                x_words = x_rows[(batch, first_tile + j)].bitcast(F32)
                 xt = xt_pool.tile([P, PASSES, 2, P], F32)
                 for g in range(PASSES):
                     for u in range(2):
@@ -179,18 +199,20 @@ def tile_causalselfattentiongqa_pa_t_kernel(tc, x, w_qkv_words, w_qkv_scales, ou
         def quantise_group(i):
             codes = mx_pool.tile([P, GROUP, PASSES, P], U32, align_bytes=64)
             planes = mx_pool.tile([P, GROUP, PASSES, P], U8, align_bytes=64)
-            for j in range(GROUP):
+            tiles = groups[i][2]
+            step = min(QUANT_TILES, tiles)
+            for j in range(0, tiles, step):
                 nc.vector.quantize_mx(
-                    out=codes[:, j].rearrange("p g r -> p (g r)").bitcast(FP8X4),
-                    scales=planes[:, j].rearrange("p g r -> p (g r)"),
-                    in_=grouped_tiles[i][:, j * D : (j + 1) * D],
+                    out=codes[:, j : j + step].rearrange("p j g r -> p (j g r)").bitcast(FP8X4),
+                    scales=planes[:, j : j + step].rearrange("p j g r -> p (j g r)"),
+                    in_=grouped_tiles[i][:, j * D : (j + step) * D],
                 )
             code_tiles[i] = codes
             plane_tiles[i] = planes
 
         def multiply_group(i):
             acc = acc_pool.tile([P, GROUP, COLS], F32)
-            for j in range(GROUP):
+            for j in range(groups[i][2]):
                 for g in range(PASSES):
                     nc.tensor.matmul_mx(
                         out=acc[:, j, :],
@@ -204,50 +226,53 @@ def tile_causalselfattentiongqa_pa_t_kernel(tc, x, w_qkv_words, w_qkv_scales, ou
             acc_tiles[i] = acc
 
         def rope_group(i):
-            store, place = divmod(i, STORE_GROUPS)
-            if place == 0:
+            batch, first_tile, tiles = groups[i]
+            store = [
+                n for n in range(len(stores))
+                if stores[n][0] == batch and stores[n][1] <= first_tile < stores[n][1] + stores[n][2]
+            ][0]
+            store_first, store_tiles = stores[store][1], stores[store][2]
+            if first_tile == store_first:
                 result = out_pool.tile([P, HEADS, STORE_TILES, DH], F32)
                 result_tiles[store] = result
             result = result_tiles[store]
-            here = slice(place * GROUP, (place + 1) * GROUP)
-            first_tile = (i % GROUPS_BATCH) * GROUP
-            acc = acc_tiles[i]
+            here = slice(first_tile - store_first, first_tile - store_first + tiles)
+            acc = acc_tiles[i][:, 0:tiles, :]
 
             nc.scalar.copy(out=result[:, ROPED_HEADS, here, :], in_=acc[:, :, ROPED_HEADS * DH : COLS])
 
-            pair_shape = [P, GROUP, ROPED_HEADS, HALF, 2]
+            pair_shape = [P, tiles, ROPED_HEADS, HALF, 2]
             pairs = acc[:, :, 0 : ROPED_HEADS * DH].rearrange("p j (h i two) -> p j h i two", h=ROPED_HEADS, two=2)
-            tiles_here = slice(first_tile, first_tile + GROUP)
-            from_even = work.tile(pair_shape, F32)
+            tiles_here = slice(first_tile, first_tile + tiles)
+            from_even = work.tile([P, GROUP, ROPED_HEADS, HALF, 2], F32)
             nc.vector.tensor_tensor(
-                out=from_even[:],
+                out=from_even[:, 0:tiles],
                 in0=pairs[:, :, :, :, 0:1].to_broadcast(pair_shape),
                 in1=table_of_even[:, tiles_here].unsqueeze(2).to_broadcast(pair_shape),
                 op=ALU.mult,
             )
-            from_odd = work.tile(pair_shape, F32)
+            from_odd = work.tile([P, GROUP, ROPED_HEADS, HALF, 2], F32)
             nc.vector.tensor_tensor(
-                out=from_odd[:],
+                out=from_odd[:, 0:tiles],
                 in0=pairs[:, :, :, :, 1:2].to_broadcast(pair_shape),
                 in1=table_of_odd[:, tiles_here].unsqueeze(2).to_broadcast(pair_shape),
                 op=ALU.mult,
             )
             nc.vector.tensor_tensor(
                 out=result[:, 0:ROPED_HEADS, here, :],
-                in0=from_even[:].rearrange("p j h i two -> p h j (i two)"),
-                in1=from_odd[:].rearrange("p j h i two -> p h j (i two)"),
+                in0=from_even[:, 0:tiles].rearrange("p j h i two -> p h j (i two)"),
+                in1=from_odd[:, 0:tiles].rearrange("p j h i two -> p h j (i two)"),
                 op=ALU.add,
             )
 
-            if place == STORE_GROUPS - 1:
-                batch, part = divmod(store, GROUPS_BATCH // STORE_GROUPS)
-                stored = slice(part * STORE_TILES, (part + 1) * STORE_TILES)
+            if first_tile + tiles == store_first + store_tiles:
+                stored = slice(store_first, store_first + store_tiles)
                 q_rows = out_0[batch, 0].rearrange("h (p a) d -> p h a d", a=TILES_BATCH)
                 k_rows = out_1[batch, 0].rearrange("(p a) d -> p a d", a=TILES_BATCH)
                 v_rows = out_2[batch, 0].rearrange("(p a) d -> p a d", a=TILES_BATCH)
-                nc.sync.dma_start(out=q_rows[:, :, stored, :], in_=result[:, 0:2, :, :])
-                nc.sync.dma_start(out=k_rows[:, stored, :], in_=result[:, 2, :, :])
-                nc.sync.dma_start(out=v_rows[:, stored, :], in_=result[:, 3, :, :])
+                nc.sync.dma_start(out=q_rows[:, :, stored, :], in_=result[:, 0:2, 0:store_tiles, :])
+                nc.sync.dma_start(out=k_rows[:, stored, :], in_=result[:, 2, 0:store_tiles, :])
+                nc.sync.dma_start(out=v_rows[:, stored, :], in_=result[:, 3, 0:store_tiles, :])
 
         transpose_group(0)
         quantise_group(0)

import math
from contextlib import ExitStack

import concourse.mybir as mybir
from concourse.masks import make_identity

F32 = mybir.dt.float32
BF16 = mybir.dt.bfloat16
I32 = mybir.dt.int32
U32 = mybir.dt.uint32
U8 = mybir.dt.uint8
FP8X4 = mybir.dt.float8_e4m3fn_x4
FP4X4 = mybir.dt.float4_e2m1fn_x4
ALU = mybir.AluOpType
ACT = mybir.ActivationFunctionType

BATCH, T, D = 4, 2048, 1024
DH = 32
HALF = DH // 2
ROPED_HEADS = 3
HEADS = 4
COLS = HEADS * DH

P = 128
K_PASS = 4 * P
PASSES = D // K_PASS
WORDS_PASS = K_PASS // 2

TILES_BATCH = T // P
GROUP = 4
STORE_TILES = 16
QUANT_TILES = 1

BATCH_GROUPS = [4, 4, 4, 4]
LAST_BATCH_GROUPS = [4, 4, 4, 4]
BATCH_LOADS = [2, 2, 2, 2, 2, 2, 2, 2]
FIRST_BATCH_LOADS = [2, 2, 2, 2, 2, 2, 2, 2]
BATCH_STORES = [16]
LAST_BATCH_STORES = [8, 4, 4]
RESULT_BUFFERS = 4

ROPE_THETA = 1e6
YARN_FACTOR = 64.0
RAMP_LOW, RAMP_HIGH = 5, 8
ATTN_FACTOR = 0.1 * math.log(YARN_FACTOR) + 1.0

ROUND = 1.5 * 2.0**23

FLOPS = 2 * BATCH * T * D * COLS


def turns_per_position(i):
    plain = ROPE_THETA ** (-i / HALF)
    ramp = min(max((i - RAMP_LOW) / (RAMP_HIGH - RAMP_LOW), 0.0), 1.0)
    return (plain * (1.0 - ramp) + plain / YARN_FACTOR * ramp) / (2.0 * math.pi)


def split_13_bits(value):
    exponent = math.floor(math.log(value) / math.log(2.0))
    step = 2.0 ** (exponent - 12)
    high = round(value / step) * step
    return high, value - high


def tile_causalselfattentiongqa_pa_t_kernel(tc, x, w_qkv_words, w_qkv_scales, out_0, out_1, out_2):
    nc = tc.nc
    with ExitStack() as ctx:
        const = ctx.enter_context(tc.tile_pool(name="const", bufs=1))
        x_pool = ctx.enter_context(tc.tile_pool(name="x", bufs=1))
        grouped_pool = ctx.enter_context(tc.tile_pool(name="grouped", bufs=3))
        mx_pool = ctx.enter_context(tc.tile_pool(name="mx", bufs=3))
        work = ctx.enter_context(tc.tile_pool(name="work", bufs=2))
        out_pool = ctx.enter_context(tc.tile_pool(name="out", bufs=RESULT_BUFFERS))
        xt_pool = ctx.enter_context(tc.psum_pool(name="xt", bufs=6))
        acc_pool = ctx.enter_context(tc.psum_pool(name="acc", bufs=2))

        def spans(batch_plans):
            found = []
            for batch in range(BATCH):
                first = 0
                for tiles in batch_plans[batch]:
                    found.append((batch, first, tiles))
                    first += tiles
                assert first == TILES_BATCH
            return found

        loads = spans([FIRST_BATCH_LOADS] + [BATCH_LOADS] * (BATCH - 1))
        groups = spans([BATCH_GROUPS] * (BATCH - 1) + [LAST_BATCH_GROUPS])
        stores = spans([BATCH_STORES] * (BATCH - 1) + [LAST_BATCH_STORES])
        GROUPS = len(groups)

        x_rows = {}

        def load_x(n):
            batch, first, tiles = loads[n]
            x_sb = x_pool.tile([P, tiles, D], BF16, name="x%d" % n)
            tokens = x[batch].rearrange("(p a) k -> p a k", a=TILES_BATCH)
            nc.sync.dma_start(out=x_sb[:], in_=tokens[:, first : first + tiles, :])
            for place in range(tiles):
                x_rows[(batch, first + place)] = x_sb[:, place, :]

        w_words = const.tile([P, PASSES, 2 * COLS], U8, align_bytes=64)
        w_planes = const.tile([P, PASSES, COLS], U8, align_bytes=64)
        nc.vector.memset(w_planes[:].bitcast(I32), 0)

        loads_before_w = len([1 for batch, first, tiles in loads if batch == 0 and first < 2 * GROUP])
        for n in range(loads_before_w):
            load_x(n)
        nc.sync.dma_start(out=w_words[:].bitcast(I32), in_=w_qkv_words.rearrange("g p n -> p g n").bitcast(I32))
        for quadrant in range(4):
            nc.sync.dma_start(
                out=w_planes[32 * quadrant : 32 * quadrant + 4].bitcast(I32),
                in_=w_qkv_scales[:, 4 * quadrant : 4 * quadrant + 4, :].rearrange("g r n -> r g n").bitcast(I32),
            )
        for n in range(loads_before_w, len(loads)):
            load_x(n)

        position_int = const.tile([P, TILES_BATCH], I32)
        nc.gpsimd.iota(position_int[:], pattern=[[1, TILES_BATCH]], base=0, channel_multiplier=TILES_BATCH)
        identity = const.tile([P, P], F32)
        make_identity(nc, identity[:])

        zero = const.tile([P, 1], F32)
        nc.vector.memset(zero[:], 0.0)
        sin_of_zero = const.tile([P, 1], F32)
        nc.scalar.activation(out=sin_of_zero[:], in_=zero[:], func=ACT.Sin)

        angle_shape = [P, TILES_BATCH, HALF]
        position = const.tile([P, TILES_BATCH], F32)
        nc.vector.tensor_copy(out=position[:], in_=position_int[:])

        def minus_fraction(out, value, shifted):
            nc.vector.tensor_scalar_add(out=shifted, in0=value, scalar1=ROUND)
            nc.vector.scalar_tensor_tensor(
                out=out, in0=shifted, scalar=ROUND, in1=value, op0=ALU.subtract, op1=ALU.subtract
            )

        coarse = const.tile(angle_shape, F32)
        for i in range(HALF):
            high, low = split_13_bits(turns_per_position(i))
            nc.vector.tensor_scalar_mul(out=coarse[:, :, i], in0=position[:], scalar1=high)
        coarse_shifted = const.tile(angle_shape, F32)
        minus_coarse = const.tile(angle_shape, F32)
        minus_fraction(minus_coarse[:], coarse[:], coarse_shifted[:])

        turns = const.tile(angle_shape, F32)
        for i in range(HALF):
            high, low = split_13_bits(turns_per_position(i))
            nc.vector.scalar_tensor_tensor(
                out=turns[:, :, i], in0=position[:], scalar=low, in1=minus_coarse[:, :, i],
                op0=ALU.mult, op1=ALU.subtract,
            )
        turns_shifted = const.tile(angle_shape, F32)
        minus_turns = const.tile(angle_shape, F32)
        minus_fraction(minus_turns[:], turns[:], turns_shifted[:])

        minus_abs = const.tile(angle_shape, F32)
        nc.vector.scalar_tensor_tensor(
            out=minus_abs[:], in0=minus_turns[:], scalar=-1.0, in1=minus_turns[:], op0=ALU.mult, op1=ALU.min
        )
        quarter_less_abs = const.tile(angle_shape, F32)
        nc.vector.tensor_scalar_add(out=quarter_less_abs[:], in0=minus_abs[:], scalar1=0.25)

        table_of_even = const.tile([P, TILES_BATCH, HALF, 2], F32)
        table_of_odd = const.tile([P, TILES_BATCH, HALF, 2], F32)

        def build_tables():
            sin = const.tile(angle_shape, F32)
            cos = const.tile(angle_shape, F32)
            nc.scalar.activation(out=sin[:], in_=minus_turns[:], func=ACT.Sin, scale=-2.0 * math.pi)
            nc.scalar.activation(out=cos[:], in_=quarter_less_abs[:], func=ACT.Sin, scale=2.0 * math.pi)
            nc.vector.tensor_scalar_mul(out=table_of_even[:, :, :, 0], in0=cos[:], scalar1=ATTN_FACTOR)
            nc.vector.tensor_scalar_mul(out=table_of_even[:, :, :, 1], in0=sin[:], scalar1=ATTN_FACTOR)
            nc.vector.tensor_scalar_mul(out=table_of_odd[:, :, :, 0], in0=sin[:], scalar1=-ATTN_FACTOR)
            nc.vector.tensor_scalar_mul(out=table_of_odd[:, :, :, 1], in0=cos[:], scalar1=ATTN_FACTOR)

        grouped_tiles = {}
        code_tiles = {}
        plane_tiles = {}
        acc_tiles = {}
        result_tiles = {}

        def transpose_group(i):
            grouped = grouped_pool.tile([P, GROUP * D], BF16, align_bytes=64)
            grouped_words = grouped[:].bitcast(F32).rearrange(
                "p (j g r u) -> p j g r u", j=GROUP, g=PASSES, u=2
            )
            batch, first_tile, tiles = groups[i]
            for j in range(tiles):
                x_words = x_rows[(batch, first_tile + j)].bitcast(F32)
                xt = xt_pool.tile([P, PASSES, 2, P], F32)
                for g in range(PASSES):
                    for u in range(2):
                        first = WORDS_PASS * g + u
                        nc.tensor.transpose(xt[:, g, u, :], x_words[:, first : WORDS_PASS * (g + 1) : 2], identity[:])
                nc.scalar.copy(out=grouped_words[:, j], in_=xt[:].rearrange("p g u r -> p g r u"))
            grouped_tiles[i] = grouped

        def quantise_group(i):
            codes = mx_pool.tile([P, GROUP, PASSES, P], U32, align_bytes=64)
            planes = mx_pool.tile([P, GROUP, PASSES, P], U8, align_bytes=64)
            tiles = groups[i][2]
            step = min(QUANT_TILES, tiles)
            for j in range(0, tiles, step):
                nc.vector.quantize_mx(
                    out=codes[:, j : j + step].rearrange("p j g r -> p (j g r)").bitcast(FP8X4),
                    scales=planes[:, j : j + step].rearrange("p j g r -> p (j g r)"),
                    in_=grouped_tiles[i][:, j * D : (j + step) * D],
                )
            code_tiles[i] = codes
            plane_tiles[i] = planes

        def multiply_group(i):
            acc = acc_pool.tile([P, GROUP, COLS], F32)
            for j in range(groups[i][2]):
                for g in range(PASSES):
                    nc.tensor.matmul_mx(
                        out=acc[:, j, :],
                        lhsT=code_tiles[i][:, j, g, :].bitcast(FP8X4),
                        lhsT_scale=plane_tiles[i][:, j, g, :],
                        rhs=w_words[:, g, :].bitcast(FP4X4),
                        rhs_scale=w_planes[:, g, :],
                        start=(g == 0),
                        stop=(g == PASSES - 1),
                    )
            acc_tiles[i] = acc

        def rope_group(i):
            batch, first_tile, tiles = groups[i]
            store = [
                n for n in range(len(stores))
                if stores[n][0] == batch and stores[n][1] <= first_tile < stores[n][1] + stores[n][2]
            ][0]
            store_first, store_tiles = stores[store][1], stores[store][2]
            if first_tile == store_first:
                result = out_pool.tile([P, HEADS, STORE_TILES, DH], F32)
                result_tiles[store] = result
            result = result_tiles[store]
            here = slice(first_tile - store_first, first_tile - store_first + tiles)
            acc = acc_tiles[i][:, 0:tiles, :]

            nc.scalar.copy(out=result[:, ROPED_HEADS, here, :], in_=acc[:, :, ROPED_HEADS * DH : COLS])

            pair_shape = [P, tiles, ROPED_HEADS, HALF, 2]
            pairs = acc[:, :, 0 : ROPED_HEADS * DH].rearrange("p j (h i two) -> p j h i two", h=ROPED_HEADS, two=2)
            tiles_here = slice(first_tile, first_tile + tiles)
            from_even = work.tile([P, GROUP, ROPED_HEADS, HALF, 2], F32)
            nc.vector.tensor_tensor(
                out=from_even[:, 0:tiles],
                in0=pairs[:, :, :, :, 0:1].to_broadcast(pair_shape),
                in1=table_of_even[:, tiles_here].unsqueeze(2).to_broadcast(pair_shape),
                op=ALU.mult,
            )
            from_odd = work.tile([P, GROUP, ROPED_HEADS, HALF, 2], F32)
            nc.vector.tensor_tensor(
                out=from_odd[:, 0:tiles],
                in0=pairs[:, :, :, :, 1:2].to_broadcast(pair_shape),
                in1=table_of_odd[:, tiles_here].unsqueeze(2).to_broadcast(pair_shape),
                op=ALU.mult,
            )
            nc.vector.tensor_tensor(
                out=result[:, 0:ROPED_HEADS, here, :],
                in0=from_even[:, 0:tiles].rearrange("p j h i two -> p h j (i two)"),
                in1=from_odd[:, 0:tiles].rearrange("p j h i two -> p h j (i two)"),
                op=ALU.add,
            )

            if first_tile + tiles == store_first + store_tiles:
                stored = slice(store_first, store_first + store_tiles)
                q_rows = out_0[batch, 0].rearrange("h (p a) d -> p h a d", a=TILES_BATCH)
                k_rows = out_1[batch, 0].rearrange("(p a) d -> p a d", a=TILES_BATCH)
                v_rows = out_2[batch, 0].rearrange("(p a) d -> p a d", a=TILES_BATCH)
                nc.sync.dma_start(out=q_rows[:, :, stored, :], in_=result[:, 0:2, 0:store_tiles, :])
                nc.sync.dma_start(out=k_rows[:, stored, :], in_=result[:, 2, 0:store_tiles, :])
                nc.sync.dma_start(out=v_rows[:, stored, :], in_=result[:, 3, 0:store_tiles, :])

        transpose_group(0)
        quantise_group(0)
        build_tables()
        transpose_group(1)
        quantise_group(1)
        multiply_group(0)
        for i in range(2, GROUPS):
            rope_group(i - 2)
            transpose_group(i)
            quantise_group(i)
            multiply_group(i - 1)
        rope_group(GROUPS - 2)
        multiply_group(GROUPS - 1)
        rope_group(GROUPS - 1)
